import numpy as np
import ml_dtypes


def mxq(x, axis, fmt="e4m3"):
    dtype, down = {"e4m3": (ml_dtypes.float8_e4m3fn, 7), "e5m2": (ml_dtypes.float8_e5m2, 14)}[fmt]
    v = np.moveaxis(np.asarray(x, np.float32).astype(ml_dtypes.bfloat16).astype(np.float64), axis, -1)
    blocks = v.reshape(v.shape[:-1] + (-1, 32))
    amax = np.abs(blocks).max(-1, keepdims=True)
    byte = np.maximum(np.where(amax > 0, np.frexp(amax)[1] - 1 + 127, 0) - down, 1)
    scale = np.exp2(byte - 127.0)
    codes = (blocks / scale).astype(np.float32).astype(dtype).astype(np.float64)
    return np.moveaxis((codes * scale).reshape(v.shape), -1, axis)


WIDE = False


def mx_kscale(k):
    if not WIDE:
        return np.ones(k)
    levels = np.array([10, -10, 5, -5, 0])
    if k % 512:
        return np.exp2(np.random.permutation(np.resize(levels, k // 32))).repeat(32)
    a = np.empty((k // 512, 16))
    for p in range(k // 512):
        a[p, :8] = np.random.permutation(np.resize(levels, 8))
        for g in range(8):
            far = levels[np.abs(levels - a[p, g]) >= 10]
            a[p, g + 8] = far[np.random.randint(len(far))]
    return np.exp2(a.ravel()).repeat(32)


BF16 = ml_dtypes.bfloat16


def bf(x):
    return np.asarray(x, np.float32).astype(BF16)


def f64(x):
    return np.asarray(x).astype(np.float64)


B, H, W, C = 128, 5, 5, 1024
PIXEL = 2
STEP = 1
EPS = 1e-6
PAD = (PIXEL - H % PIXEL) % PIXEL
HP = H + PAD
R = HP // PIXEL
K1 = PIXEL * C
F = C // 2


def layer_norm(v, g, b):
    m = v.mean(-1, keepdims=True)
    var = np.square(v - m).mean(-1, keepdims=True)
    return (v - m) / np.sqrt(var + EPS) * g + b


def draw0():
    s = mx_kscale(C)
    t = mx_kscale(F)
    return {
        "x": bf(np.random.standard_normal((B, H, W, C)) * s),
        "wh1": bf(np.random.standard_normal((K1, F)) / np.sqrt(K1) / np.tile(s, PIXEL)[:, None]),
        "gh": bf((1.0 + 0.1 * np.random.standard_normal(F)) * t),
        "bh": bf(0.2 * np.random.standard_normal(F) * t),
        "wh2": bf(np.random.standard_normal((F, K1)) / np.sqrt(F) / t[:, None]),
        "bh2": bf(0.3 * np.random.standard_normal(K1)),
    }


def core(x, wh1, gh, bh, wh2, bh2):
    r = np.roll(f64(x), STEP, axis=1)
    r = np.concatenate([r[:, -PAD:], r], axis=1)
    z = r.reshape(B, PIXEL, R, W, C).transpose(0, 2, 3, 1, 4).reshape(B, R, W, K1)
    u = mxq(z, 3, "e4m3") @ mxq(f64(wh1), 0, "e4m3")
    hid = np.maximum(layer_norm(u, f64(gh), f64(bh)), 0.0)
    y = (mxq(hid, 3, "e4m3") @ mxq(f64(wh2), 0, "e4m3")) + f64(bh2)
    y = y.reshape(B, R, W, PIXEL, C).transpose(0, 3, 1, 2, 4).reshape(B, HP, W, C)[:, PAD:]
    return np.roll(y, -STEP, axis=1)


def e4m3fn_bytes(y):
    return np.clip(np.asarray(y, np.float64), -448.0, 448.0).astype(np.float32).astype(ml_dtypes.float8_e4m3fn).view(np.uint8)


def e4m3fn_values(b):
    return np.asarray(b, np.uint8).view(ml_dtypes.float8_e4m3fn).astype(np.float64)


def setup_inputs():
    d = draw0()
    x0 = np.asarray(d['x']).astype(np.float64)
    s = (np.max(np.abs(x0), axis=(0, 1, 2), keepdims=True) / 448.0).astype(np.float32)
    out = {}
    for k, v in d.items():
        if k == 'x':
            out['x_bytes'] = e4m3fn_bytes(x0 / s.astype(np.float64))
            out['x_scale'] = s
        else:
            out[k] = v
    return out


def reference(x_bytes, x_scale, wh1, gh, bh, wh2, bh2):
    return core(e4m3fn_values(x_bytes) * x_scale.astype(np.float64), wh1, gh, bh, wh2, bh2)

from contextlib import ExitStack

import concourse.mybir as mybir
from concourse.masks import make_identity

F32 = mybir.dt.float32
BF16 = mybir.dt.bfloat16
U32 = mybir.dt.uint32
U8 = mybir.dt.uint8
E4M3 = mybir.dt.float8_e4m3fn
FP8X4 = mybir.dt.float8_e4m3fn_x4
ALU = mybir.AluOpType
ACT = mybir.ActivationFunctionType

B, H, W, C = 128, 5, 5, 1024
F = 512
K1 = 2 * C
EPS = 1e-6
FLOPS = 2 * B * W * F * (3 * K1 + 5 * C)

REGION = {0: (3, 1, None, 1), 1: (4, 2, 4, 2), 2: (0, 3, 0, 3)}
STEPS = [(w, j, rows) for w in range(W) for j, rows in ((0, (3, 1)), (2, (0,)), (1, (4, 2)))]
XS_A = {k: 1 for k in range(15)}
XS_B = {0: 1, 1: 1, 2: 1}
XS_W = 1
W_AT = {0: [("b", 2)], 1: [("b", 3)], 2:[("b", 0)],3:[("b", 1)]}
WQ_AT = {0: [], 1: [("b", 2)], 2: [("b",3),("b", 0)],3:[("b", 1)]}


def tile_hiremodule_pa_kernel(tc, x_bytes, x_scale, wh1, gh, bh, wh2, bh2, out):
    nc = tc.nc
    with ExitStack() as ctx:
        keep = ctx.enter_context(tc.tile_pool(name="keep", bufs=1))
        work = ctx.enter_context(tc.tile_pool(name="work", bufs=2))
        psum = ctx.enter_context(tc.psum_pool(name="psum", bufs=2))

        w_raw = {}

        def load_weights(key, src):
            t = keep.tile([128, 4, 512], BF16, name="raw_%s_%d" % key)
            nc.sync.dma_start(out=t[:], in_=src)
            w_raw[key] = t

        def load_wh1(g):
            load_weights(("a", g), wh1[512 * g : 512 * (g + 1), :].rearrange("(p j) n -> p j n", j=4))

        def load_wh2(q):
            load_weights(("b", q), wh2[:, 512 * q : 512 * (q + 1)].rearrange("(p j) n -> p j n", j=4))

        x_loaded = {}

        def load_x(w0, w1):
            t = keep.tile([B, H, (w1 - w0) * C], U8, name="xb%d" % w0)
            nc.sync.dma_start(out=t[:], in_=x_bytes[:, :, w0:w1, :].rearrange("b h w c -> b h (w c)"))
            for w in range(w0, w1):
                for h in range(H):
                    x_loaded[w, h] = t[:, h, (w - w0) * C : (w - w0 + 1) * C]

        load_wh1(0)
        scale_bc = keep.tile([128, C], F32)
        nc.sync.dma_start(out=scale_bc[:], in_=x_scale.rearrange("a b c k -> (a b c k)").partition_broadcast(128))
        load_x(0, 1)
        for g in range(1, 4):
            load_wh1(g)
        gain_raw = keep.tile([128, 4], BF16)
        nc.sync.dma_start(out=gain_raw[:], in_=gh.rearrange("(p t) -> p t", t=4))
        beta_raw = keep.tile([128, 4], BF16)
        nc.sync.dma_start(out=beta_raw[:], in_=bh.rearrange("(p t) -> p t", t=4))
        load_x(1, 3)
        load_wh2(2)
        load_wh2(3)
        load_x(3, 5)
        bias_bc = keep.tile([128, K1], BF16)
        nc.sync.dma_start(out=bias_bc[:], in_=bh2.partition_broadcast(128))
        load_wh2(0)
        load_wh2(1)

        warm = keep.tile([128, 1], F32)
        nc.vector.memset(warm[:], 0.0)
        nc.scalar.activation(warm[:], warm[:], ACT.Relu)
        ident = keep.tile([128, 128], F32)
        make_identity(nc, ident[:])
        minus_half = keep.tile([128, 1], F32)
        nc.gpsimd.memset(minus_half[:], -0.5)
        gain = keep.tile([128, 4], F32)
        nc.gpsimd.tensor_copy(out=gain[:], in_=gain_raw[:])
        beta = keep.tile([128, 4], F32)
        nc.gpsimd.tensor_copy(out=beta[:], in_=beta_raw[:])

        w_grouped, w_codes, w_scales = {}, {}, {}

        def interleave_weights(copy, key):
            t = work.tile([128, 512, 4], BF16, name="w_grouped", bufs=3, align_bytes=64)
            copy(out=t[:], in_=w_raw[key][:].rearrange("p j n -> p n j"))
            w_grouped[key] = t

        def quantize_weights(key):
            codes = keep.tile([128, 512], U32, name="wc_%s_%d" % key, align_bytes=64)
            scales = keep.tile([128, 512], U8, name="ws_%s_%d" % key, align_bytes=64)
            nc.vector.quantize_mx(
                out=codes[:].bitcast(FP8X4), scales=scales[:], in_=w_grouped[key][:].rearrange("p n j -> p (n j)")
            )
            w_codes[key], w_scales[key] = codes, scales

        x_order = [(w, h) for w, j, rows in STEPS for h in rows]
        x_scaled = {}
        pending = list(x_order)

        def scale_x(count):
            for i in range(min(count, len(pending))):
                w, h = pending.pop(0)
                t = work.tile([128, C], BF16, name="xs", bufs=20, align_bytes=64)
                nc.vector.tensor_tensor(
                    out=t[:], in0=x_loaded[w, h].bitcast(E4M3), in1=scale_bc[:], op=ALU.mult
                )
                x_scaled[w, h] = t

        x_grouped, x_codes, x_planes, x_place = {}, {}, {}, {}

        def turn_x(s):
            w, j, rows = STEPS[s]
            t = work.tile([128, 2 * C], BF16, name="xg", bufs=3, align_bytes=64)
            for i, h in enumerate(rows):
                while (w, h) not in x_scaled:
                    scale_x(1)
                words = x_scaled[w, h][:].bitcast(F32)
                xt = psum.tile([128, 2, 2, 128], F32, name="tp", bufs=3)
                for g in range(2):
                    for u in range(2):
                        nc.tensor.transpose(xt[:, g, u, :], words[:, 256 * g + u : 256 * (g + 1) : 2], ident[:])
                nc.scalar.copy(
                    out=t[:, C * i : C * (i + 1)].bitcast(F32).rearrange("p (g r u) -> p g r u", g=2, u=2),
                    in_=xt[:].rearrange("p g u r -> p g r u"),
                )
            x_grouped[s] = t

        def quantize_x(s):
            w, j, rows = STEPS[s]
            n = 256 * len(rows)
            codes = work.tile([128, 512], U32, name="xc", bufs=5, align_bytes=64)
            planes = work.tile([128, 512], U8, name="xp", bufs=5, align_bytes=64)
            nc.vector.quantize_mx(
                out=codes[:, :n].bitcast(FP8X4), scales=planes[:, :n], in_=x_grouped[s][:, : 4 * n]
            )
            for i, h in enumerate(rows):
                x_place[w, h] = (codes, planes, 256 * i)

        u_tiles = {}

        def multiply_1(s):
            w, j, rows = STEPS[s]
            u = psum.tile([128, F], F32, name="u", bufs=2)
            for half in range(2):
                codes, planes, base = x_place[w, REGION[j][half]]
                for g in range(2):
                    k = 2 * half + g
                    cols = slice(base + 128 * g, base + 128 * (g + 1))
                    nc.tensor.matmul_mx(
                        out=u[:],
                        lhsT=codes[:, cols].bitcast(FP8X4),
                        lhsT_scale=planes[:, cols],
                        rhs=w_codes["a", k][:].bitcast(FP8X4),
                        rhs_scale=w_scales["a", k][:],
                        start=(k == 0),
                        stop=(k == 3),
                    )
            u_tiles[s] = u

        norms = {}

        stats_tiles = {}

        def statistics(s):
            stats = work.tile([128, 6], F32, name="stats")
            nc.vector.bn_stats(out=stats[:], in_=u_tiles[s][:])
            stats_tiles[s] = stats

        def moments(s):
            stats = stats_tiles[s]
            mv = work.tile([128, 2], F32, name="mv")
            nc.vector.bn_aggr(out=mv[:], in_=stats[:])
            ve = work.tile([128, 1], F32, name="ve")
            nc.gpsimd.tensor_scalar(
                out=ve[:], in0=mv[:, 1:2], scalar1=1.0, scalar2=EPS, op0=ALU.mult, op1=ALU.add
            )
            rstd = work.tile([128, 1], F32, name="rstd")
            nc.gpsimd.tensor_tensor(out=rstd[:], in0=ve[:], in1=minus_half[:], op=ALU.pow)
            shift = work.tile([128, 1], F32, name="shift")
            nc.gpsimd.tensor_scalar(
                out=shift[:], in0=mv[:, 0:1], scalar1=rstd[:, 0:1], scalar2=-1.0, op0=ALU.mult, op1=ALU.mult
            )
            norms[s] = (rstd, shift)

        n_tiles = {}

        def normalise(s):
            rstd, shift = norms[s]
            n = work.tile([128, 4, 128], F32, name="n", align_bytes=64)
            nc.scalar.activation(
                n[:], u_tiles[s][:].rearrange("p (m t) -> p t m", t=4), ACT.Identity, bias=shift[:, 0:1], scale=rstd[:, 0:1]
            )
            n_tiles[s] = n

        h_turned, h_grouped, h_codes = {}, {}, {}

        def turn_n(s):
            ht = psum.tile([128, 2, 2, 128], F32, name="tp", bufs=3)
            for t in range(4):
                nc.tensor.transpose(ht[:, t // 2, t % 2, :], n_tiles[s][:, t, :], ident[:])
            h_turned[s] = ht

        def gain_bias_relu(s):
            hp = work.tile([128, 4, 128], BF16, name="hp", align_bytes=64)
            for t in range(4):
                nc.scalar.activation(
                    hp[:, t, :], h_turned[s][:, t // 2, t % 2, :], ACT.Relu, bias=beta[:, t : t + 1], scale=gain[:, t : t + 1]
                )
            hg = work.tile([128, 128, 4], BF16, name="hg", bufs=3, align_bytes=64)
            nc.scalar.copy(out=hg[:], in_=hp[:].rearrange("p t r -> p r t"))
            h_grouped[s] = hg

        def quantize_h(s):
            codes = work.tile([128, 128], U32, name="hc", bufs=3, align_bytes=64)
            planes = work.tile([128, 128], U8, name="hs", bufs=3, align_bytes=64)
            nc.vector.quantize_mx(
                out=codes[:].bitcast(FP8X4), scales=planes[:], in_=h_grouped[s][:].rearrange("p r t -> p (r t)")
            )
            h_codes[s] = (codes, planes)

        def quarters(s):
            j = STEPS[s][1]
            return [q for q in range(4) if REGION[j][2 + q // 2] is not None]

        y_tiles, o_tiles = {}, {}

        def multiply_2(s, some):
            for q in quarters(s)[some]:
                codes, planes = h_codes[s]
                y = psum.tile([128, 512], F32, name="y", bufs=3)
                nc.tensor.matmul_mx(
                    out=y[:],
                    lhsT=codes[:].bitcast(FP8X4),
                    lhsT_scale=planes[:],
                    rhs=w_codes["b", q][:].bitcast(FP8X4),
                    rhs_scale=w_scales["b", q][:],
                    start=True,
                    stop=True,
                )
                y_tiles[s, q] = y

        def add_bias(s, some):
            w, j, rows = STEPS[s]
            for q in quarters(s)[some]:
                if q % 2 == 0:
                    o_new = work.tile([128, C], F32, name="o", bufs=5)
                    o_tiles[s] = o_new
                o = o_tiles[s]
                cols = slice(512 * (q % 2), 512 * (q % 2 + 1))
                nc.vector.tensor_tensor(
                    out=o[:, cols], in0=y_tiles[s, q][:], in1=bias_bc[:, 512 * q : 512 * (q + 1)], op=ALU.add
                )
                if q % 2 == 1:
                    nc.sync.dma_start(out=out[:, REGION[j][2 + q // 2], w, :], in_=o[:])

        N = len(STEPS)
        with tc.manual_schedule():
            interleave_weights(nc.vector.tensor_copy, ("a", 0))
            interleave_weights(nc.scalar.copy, ("a", 1))
            quantize_weights(("a", 0))
            scale_x(4)
            turn_x(0)
            quantize_weights(("a", 1))
            interleave_weights(nc.scalar.copy, ("a", 2))
            scale_x(2)
            interleave_weights(nc.scalar.copy, ("a", 3))
            quantize_weights(("a", 2))
            scale_x(2)
            turn_x(1)
            quantize_weights(("a", 3))
            for k in range(N + 3):
                live2 = 0 <= k - 3 < N
                if live2:
                    quantize_h(k - 3)
                    multiply_2(k - 3, slice(0, 3))
                if k < N:
                    quantize_x(k)
                    multiply_1(k)
                if 0 <= k - 1 < N:
                    normalise(k - 1)
                scale_x(XS_A.get(k, 0))
                if live2:
                    add_bias(k - 3, slice(0, 1))
                    multiply_2(k - 3, slice(3, 4))
                    add_bias(k - 3, slice(1, 2))
                for key in W_AT.get(k, ()):
                    interleave_weights(nc.scalar.copy, key)
                if 0 <= k - 1 < N:
                    turn_n(k - 1)
                    gain_bias_relu(k - 1)
                if k + 2 < N:
                    turn_x(k + 2)
                if live2:
                    add_bias(k - 3, slice(2, 3))
                if k < N:
                    statistics(k)
                for key in WQ_AT.get(k, ()):
                    scale_x(XS_W)
                    quantize_weights(key)
                scale_x(XS_B.get(k, 0))
                if live2:
                    add_bias(k - 3, slice(3, 4))
                if k < N:
                    moments(k)
